import numpy as np
import ml_dtypes


def mxq(x, axis, fmt="e4m3"):
    dtype, down = {"e4m3": (ml_dtypes.float8_e4m3fn, 7), "e5m2": (ml_dtypes.float8_e5m2, 14)}[fmt]
    v = np.moveaxis(np.asarray(x, np.float32).astype(ml_dtypes.bfloat16).astype(np.float64), axis, -1)
    blocks = v.reshape(v.shape[:-1] + (-1, 32))
    amax = np.abs(blocks).max(-1, keepdims=True)
    byte = np.maximum(np.where(amax > 0, np.frexp(amax)[1] - 1 + 127, 0) - down, 1)
    scale = np.exp2(byte - 127.0)
    codes = (blocks / scale).astype(np.float32).astype(dtype).astype(np.float64)
    return np.moveaxis((codes * scale).reshape(v.shape), -1, axis)


WIDE = False


def mx_kscale(k):
    if not WIDE:
        return np.ones(k)
    levels = np.array([10, -10, 5, -5, 0])
    a = np.random.permutation(np.resize(levels, k // 512 * 4)).reshape(k // 512, 4)
    idx = np.arange(k)
    return np.exp2(a[idx // 512, idx % 128 // 32])


BF16 = ml_dtypes.bfloat16


def bf(x):
    return np.asarray(x, np.float32).astype(BF16)


def f64(x):
    return np.asarray(x).astype(np.float64)


E2M1 = np.array([0.0, 0.5, 1.0, 1.5, 2.0, 3.0, 4.0, 6.0, -0.0, -0.5, -1.0, -1.5, -2.0, -3.0, -4.0, -6.0])


def pack_weight(w, fmt):
    k, n = w.shape
    w = f64(bf(w)).reshape(k // 32, 32, n)
    amax = np.abs(w).max(1)
    if fmt == "e4m3":
        byte = np.frexp(amax)[1] - 1 + 127 - 7
    else:
        mant, ex = np.frexp(amax / 6.0)
        byte = np.where(mant > 0.5, ex, ex - 1) + 127
    byte = np.clip(np.where(amax > 0, byte, 1), 1, 254)
    scaled = (w * np.exp2(127.0 - byte)[:, None, :]).reshape(k, n).astype(np.float32)
    by_word = np.ascontiguousarray(scaled.reshape(k // 512, 128, 4, n).transpose(0, 1, 3, 2))
    if fmt == "e4m3":
        words = by_word.astype(ml_dtypes.float8_e4m3fn).view(np.uint8)
    else:
        c = by_word.astype(ml_dtypes.float4_e2m1fn).view(np.uint8) & 0xF
        words = c[..., 0::2] | (c[..., 1::2] << 4)
    return np.ascontiguousarray(words), np.ascontiguousarray(byte.astype(np.uint8).reshape(k // 512, 16, n))


def unpack_weight(words, scales, fmt):
    g, p, n, _ = words.shape
    if fmt == "e4m3":
        vals = np.ascontiguousarray(words).view(ml_dtypes.float8_e4m3fn).astype(np.float64)
    else:
        nib = np.empty((g, p, n, 4), np.uint8)
        nib[..., 0::2] = words & 0xF
        nib[..., 1::2] = words >> 4
        vals = E2M1[nib]
    vals = vals * np.repeat(np.exp2(scales.astype(np.float64) - 127.0), 8, axis=1)[..., None]
    return vals.transpose(0, 1, 3, 2).reshape(g * 512, n)


B, T, N, DH, D = 4, 1024, 16, 32, 512
KC = N * DH


def setup_inputs():
    r = np.random.standard_normal
    s = mx_kscale(D)
    t = mx_kscale(KC).reshape(N, DH)
    x = bf(r((B, T, D)) * s)
    wc_stack = r((N, D, DH)) / np.sqrt(D) / s[None, :, None] * t[:, None, :]
    wc_words, wc_scales = pack_weight(wc_stack.reshape(-1, DH), "e4m3")
    b_c = bf(0.1 * r((N, DH)) * t)
    w_k = bf(1.3 / np.sqrt(KC) * r((N, DH, DH, DH)) / t[:, None, None, :])
    return {"normalized_resid_pre": x,
            "W_C_words": wc_words,
            "W_C_scales": wc_scales,
            "b_C": b_c,
            "W_K": w_k}


def reference(normalized_resid_pre, W_C_words, W_C_scales, b_C, W_K):
    x = f64(normalized_resid_pre)
    wc = unpack_weight(W_C_words, W_C_scales, "e4m3").reshape(N, D, DH).transpose(1, 0, 2).reshape(D, KC)
    c = (mxq(x, 2, "e4m3") @ wc) + f64(b_C).reshape(KC)
    wk = f64(W_K).transpose(0, 3, 1, 2).reshape(KC, DH * DH)
    step1 = mxq(c, 2, "e4m3") @ mxq(wk, 0, "e4m3")
    return step1.reshape(B, T, DH, DH)

@@ -1,0 +1,211 @@
+from contextlib import ExitStack
+
+import concourse.mybir as mybir
+from concourse.masks import make_identity
+
+F32 = mybir.dt.float32
+BF16 = mybir.dt.bfloat16
+I32 = mybir.dt.int32
+U32 = mybir.dt.uint32
+U8 = mybir.dt.uint8
+FP8X4 = mybir.dt.float8_e4m3fn_x4
+ADD = mybir.AluOpType.add
+
+P = 128
+PACK = 4
+TOKENS = 4096
+D = 512
+HEADS = 16
+DH = 32
+KC = HEADS * DH
+IJ = DH * DH
+TILES = TOKENS // P
+GROUP = 4
+GROUPS = TILES // GROUP
+SUB = DH // PACK
+N_OUT = 512
+IJ_PER_ROW = IJ // P
+
+FLOPS = 2 * TOKENS * D * KC + 2 * TOKENS * KC * IJ
+
+
+def tile_trittentioncube_pa_t_e_kernel(tc, x, wc_words, wc_scales, b_c, w_k, out):
+    nc = tc.nc
+    with ExitStack() as ctx:
+        keep = ctx.enter_context(tc.tile_pool(name="keep", bufs=1))
+        x_pool = ctx.enter_context(tc.tile_pool(name="x", bufs=GROUPS))
+        stage = ctx.enter_context(tc.tile_pool(name="stage", bufs=2))
+        codes = ctx.enter_context(tc.tile_pool(name="codes", bufs=3))
+        res_pool = ctx.enter_context(tc.tile_pool(name="res", bufs=4))
+        psum = ctx.enter_context(tc.psum_pool(name="psum", bufs=2))
+
+        x_rows = x.rearrange("b r d -> (b r) d").rearrange("(p s) d -> p s d", s=TILES)
+        out_rows = out.rearrange("b r i j -> (b r) (i j)").rearrange("(p s) c -> p s c", s=TILES)
+
+        x_sb = {}
+
+        def load_x(g):
+            x_tile = x_pool.tile([P, GROUP, D], BF16)
+            nc.sync.dma_start(out=x_tile[:], in_=x_rows[:, g * GROUP : (g + 1) * GROUP, :])
+            x_sb[g] = x_tile
+
+        wcs_raw = keep.tile([P, HEADS, DH], U8, align_bytes=64)
+        nc.vector.memset(wcs_raw[:].rearrange("p g n -> p (g n)").bitcast(I32), 0)
+        ident = keep.tile([P, P], F32)
+        make_identity(nc, ident[:])
+
+        load_x(0)
+        wc_raw = keep.tile([P, HEADS, DH], I32)
+        nc.sync.dma_start(
+            out=wc_raw[:],
+            in_=wc_words.rearrange("g p n t -> g p (n t)").bitcast(I32).rearrange("g p n -> p g n"),
+        )
+        scale_words = wc_scales.bitcast(I32)
+        for quad in range(4):
+            nc.sync.dma_start(
+                out=wcs_raw[32 * quad : 32 * quad + 4].bitcast(I32),
+                in_=scale_words[:, 4 * quad : 4 * quad + 4, :].rearrange("g r w -> r g w"),
+            )
+        bias_rows = keep.tile([P, HEADS, SUB], BF16)
+        nc.vector.memset(bias_rows[:], 0.0)
+        nc.sync.dma_start(out=bias_rows[0:PACK], in_=b_c.rearrange("n (t i) -> t n i", i=SUB))
+        wk_raw = keep.tile([P, HEADS, IJ_PER_ROW, DH], BF16)
+        nc.sync.dma_start(
+            out=wk_raw[:].rearrange("p n c k -> p n (c k)"),
+            in_=w_k.rearrange("n i j k -> n (i j) k").rearrange("n (r c) k -> r n (c k)", c=IJ_PER_ROW),
+        )
+        for g in range(1, GROUPS):
+            load_x(g)
+
+        wc_codes = keep.tile([P, PACK, HEADS, SUB], I32, align_bytes=64)
+        nc.vector.tensor_copy(out=wc_codes[:], in_=wc_raw[:].rearrange("p g (t i) -> p t g i", t=PACK))
+        wc_planes = keep.tile([P, PACK, HEADS, SUB], U8, align_bytes=64)
+        nc.vector.tensor_copy(
+            out=wc_planes[:].bitcast(I32),
+            in_=wcs_raw[:].bitcast(I32).rearrange("p g (t w) -> p t g w", t=PACK),
+        )
+        bias_rows_f32 = keep.tile([P, P], F32)
+        nc.vector.tensor_copy(out=bias_rows_f32[:], in_=bias_rows[:].rearrange("p n i -> p (n i)"))
+        bias_t = psum.tile([P, P], F32, tag="c_ps")
+        nc.tensor.transpose(bias_t[:], bias_rows_f32[:], ident[:])
+        bias = keep.tile([P, PACK], F32)
+        nc.vector.tensor_copy(out=bias[:], in_=bias_t[:, 0:PACK])
+
+        x_q = {}
+        c_q = {}
+
+        def transpose_x(g):
+            x_grouped = stage.tile([P, GROUP, P, PACK], BF16, align_bytes=64)
+            grouped_words = x_grouped[:].bitcast(F32)
+            for half in range(GROUP // 2):
+                x_t = psum.tile([P, 2, 2, P], F32, tag="x_t")
+                for a in range(2):
+                    words = x_sb[g][:, 2 * half + a, :].bitcast(F32)
+                    for u in range(2):
+                        nc.tensor.transpose(x_t[:, a, u, :], words[:, u : D // 2 : 2], ident[:])
+                nc.vector.tensor_copy(
+                    out=grouped_words[:, 2 * half : 2 * half + 2, :, :],
+                    in_=x_t[:].rearrange("p a u r -> p a r u"),
+                )
+            return x_grouped
+
+        def quantise(grouped, held, g, label):
+            q_codes = codes.tile([P, GROUP * P], U32, align_bytes=64, tag=label + "_codes", name=label + "_codes")
+            q_scales = codes.tile([P, GROUP * P], U8, align_bytes=64, tag=label + "_scales", name=label + "_scales")
+            nc.vector.quantize_mx(
+                out=q_codes[:].bitcast(FP8X4),
+                scales=q_scales[:],
+                in_=grouped[:].rearrange("p a r t -> p (a r t)"),
+            )
+            held[g] = (q_codes, q_scales)
+
+        def project(g):
+            x_codes, x_scales = x_q[g]
+            c_grouped = stage.tile([P, GROUP, P, PACK], BF16, align_bytes=64)
+            for a in range(GROUP):
+                cols = slice(a * P, (a + 1) * P)
+                c_ps = psum.tile([P, PACK, P], F32, tag="c_ps")
+                for t in range(PACK):
+                    nc.tensor.matmul_mx(
+                        out=c_ps[:, t, :],
+                        lhsT=wc_codes[:, t].rearrange("p g i -> p (g i)").bitcast(FP8X4),
+                        lhsT_scale=wc_planes[:, t].rearrange("p g i -> p (g i)"),
+                        rhs=x_codes[:, cols].bitcast(FP8X4),
+                        rhs_scale=x_scales[:, cols],
+                        start=True,
+                        stop=True,
+                    )
+                nc.vector.tensor_tensor(
+                    out=c_grouped[:, a],
+                    in0=c_ps[:].rearrange("p t r -> p r t"),
+                    in1=bias[:].unsqueeze(1).to_broadcast([P, P, PACK]),
+                    op=ADD,
+                )
+            return c_grouped
+
+        def contract(g):
+            c_codes, c_scales = c_q[g]
+            for pair in range(GROUP // 2):
+                res = res_pool.tile([P, 2, IJ], F32)
+                for a in range(2):
+                    cols = slice((2 * pair + a) * P, (2 * pair + a + 1) * P)
+                    for h in range(IJ // N_OUT):
+                        o_cols = slice(h * N_OUT, (h + 1) * N_OUT)
+                        o_ps = psum.tile([P, N_OUT], F32, tag="o_ps", bufs=4)
+                        nc.tensor.matmul_mx(
+                            out=o_ps[:],
+                            lhsT=c_codes[:, cols].bitcast(FP8X4),
+                            lhsT_scale=c_scales[:, cols],
+                            rhs=wk_codes[:, o_cols].bitcast(FP8X4),
+                            rhs_scale=wk_scales[:, o_cols],
+                            start=True,
+                            stop=True,
+                        )
+                        nc.scalar.copy(out=res[:, a, o_cols], in_=o_ps[:])
+                first = g * GROUP + 2 * pair
+                nc.sync.dma_start(out=out_rows[:, first : first + 2, :], in_=res[:])
+
+        x_grouped_0 = transpose_x(0)
+        quantise(x_grouped_0, x_q, 0, "x")
+
+        wk_sorted = keep.tile([P, IJ_PER_ROW, 2, HEADS, SUB, 2], BF16)
+        for c in range(IJ_PER_ROW):
+            nc.vector.tensor_copy(
+                out=wk_sorted[:, c],
+                in_=wk_raw[:, :, c, :].rearrange("p n (u e i) -> p u n i e", u=2, e=2),
+            )
+        wk_grouped = keep.tile([P, P, IJ_PER_ROW, PACK], BF16, align_bytes=64)
+        wk_grouped_words = wk_grouped[:].bitcast(F32)
+        for b in range(IJ_PER_ROW // 2):
+            wk_t = psum.tile([P, 2, 2, P], F32, tag="o_ps", bufs=4)
+            for c2 in range(2):
+                for u in range(2):
+                    nc.tensor.transpose(
+                        wk_t[:, c2, u, :],
+                        wk_sorted[:, 2 * b + c2, u].rearrange("p n i e -> p (n i e)").bitcast(F32),
+                        ident[:],
+                    )
+            nc.scalar.copy(
+                out=wk_grouped_words[:, :, 2 * b : 2 * b + 2, :],
+                in_=wk_t[:].rearrange("p c u r -> p r c u"),
+            )
+        wk_codes = keep.tile([P, IJ], U32, align_bytes=64)
+        wk_scales = keep.tile([P, IJ], U8, align_bytes=64)
+        nc.vector.quantize_mx(
+            out=wk_codes[:].bitcast(FP8X4),
+            scales=wk_scales[:],
+            in_=wk_grouped[:].rearrange("p r c t -> p (r c t)"),
+        )
+
+        x_grouped_1 = transpose_x(1)
+        c_grouped_0 = project(0)
+        quantise(x_grouped_1, x_q, 1, "x")
+        quantise(c_grouped_0, c_q, 0, "c")
+        for g in range(GROUPS):
+            x_next = transpose_x(g + 2) if g + 2 < GROUPS else None
+            c_next = project(g + 1) if g + 1 < GROUPS else None
+            if x_next is not None:
+                quantise(x_next, x_q, g + 2, "x")
+            if c_next is not None:
+                quantise(c_next, c_q, g + 1, "c")
+            contract(g)

@@ -22,8 +22,10 @@ IJ = DH * DH
 TILES = TOKENS // P
 GROUP = 4
 GROUPS = TILES // GROUP
+PAIRS = TILES // 2
 SUB = DH // PACK
 N_OUT = 512
+HALVES = IJ // N_OUT
 IJ_PER_ROW = IJ // P
 
 FLOPS = 2 * TOKENS * D * KC + 2 * TOKENS * KC * IJ
@@ -34,10 +36,11 @@ def tile_trittentioncube_pa_t_e_kernel(tc, x, wc_words, wc_scales, b_c, w_k, out
     with ExitStack() as ctx:
         keep = ctx.enter_context(tc.tile_pool(name="keep", bufs=1))
         x_pool = ctx.enter_context(tc.tile_pool(name="x", bufs=GROUPS))
-        stage = ctx.enter_context(tc.tile_pool(name="stage", bufs=2))
-        codes = ctx.enter_context(tc.tile_pool(name="codes", bufs=3))
+        stage = ctx.enter_context(tc.tile_pool(name="stage", bufs=3))
+        codes = ctx.enter_context(tc.tile_pool(name="codes", bufs=4))
         res_pool = ctx.enter_context(tc.tile_pool(name="res", bufs=4))
         psum = ctx.enter_context(tc.psum_pool(name="psum", bufs=2))
+        ctx.enter_context(tc.manual_schedule())
 
         x_rows = x.rearrange("b r d -> (b r) d").rearrange("(p s) d -> p s d", s=TILES)
         out_rows = out.rearrange("b r i j -> (b r) (i j)").rearrange("(p s) c -> p s c", s=TILES)
@@ -51,6 +54,8 @@ def tile_trittentioncube_pa_t_e_kernel(tc, x, wc_words, wc_scales, b_c, w_k, out
 
         wcs_raw = keep.tile([P, HEADS, DH], U8, align_bytes=64)
         nc.vector.memset(wcs_raw[:].rearrange("p g n -> p (g n)").bitcast(I32), 0)
+        bias_rows = keep.tile([P, HEADS, SUB], BF16)
+        nc.vector.memset(bias_rows[:], 0.0)
         ident = keep.tile([P, P], F32)
         make_identity(nc, ident[:])
 
@@ -66,8 +71,6 @@ def tile_trittentioncube_pa_t_e_kernel(tc, x, wc_words, wc_scales, b_c, w_k, out
                 out=wcs_raw[32 * quad : 32 * quad + 4].bitcast(I32),
                 in_=scale_words[:, 4 * quad : 4 * quad + 4, :].rearrange("g r w -> r g w"),
             )
-        bias_rows = keep.tile([P, HEADS, SUB], BF16)
-        nc.vector.memset(bias_rows[:], 0.0)
         nc.sync.dma_start(out=bias_rows[0:PACK], in_=b_c.rearrange("n (t i) -> t n i", i=SUB))
         wk_raw = keep.tile([P, HEADS, IJ_PER_ROW, DH], BF16)
         nc.sync.dma_start(
@@ -76,6 +79,96 @@ def tile_trittentioncube_pa_t_e_kernel(tc, x, wc_words, wc_scales, b_c, w_k, out
         )
         for g in range(1, GROUPS):
             load_x(g)
+
+        x_grouped = {}
+        x_q = {}
+        c_banks = {}
+        c_grouped = {}
+        c_q = {}
+
+        def transpose_x(g):
+            grouped = stage.tile([P, GROUP, P, PACK], BF16, align_bytes=64, name="x_grouped")
+            grouped_words = grouped[:].bitcast(F32)
+            for half in range(GROUP // 2):
+                x_t = psum.tile([P, 2, 2, P], F32, tag="x_t")
+                for a in range(2):
+                    words = x_sb[g][:, 2 * half + a, :].bitcast(F32)
+                    for u in range(2):
+                        nc.tensor.transpose(x_t[:, a, u, :], words[:, u : D // 2 : 2], ident[:])
+                nc.scalar.copy(
+                    out=grouped_words[:, 2 * half : 2 * half + 2, :, :],
+                    in_=x_t[:].rearrange("p a u r -> p a r u"),
+                )
+            x_grouped[g] = grouped
+
+        def quantise(grouped, tiles, label):
+            q_codes = codes.tile([P, tiles * P], U32, align_bytes=64, name=label + "_codes")
+            q_scales = codes.tile([P, tiles * P], U8, align_bytes=64, name=label + "_scales")
+            nc.vector.quantize_mx(
+                out=q_codes[:].bitcast(FP8X4),
+                scales=q_scales[:],
+                in_=grouped[:].rearrange("p a r t -> p (a r t)"),
+            )
+            return q_codes, q_scales
+
+        def quantise_x(g):
+            x_q[g] = quantise(x_grouped[g], GROUP, "x")
+
+        def project(j):
+            x_codes, x_scales = x_q[j // 2]
+            c_banks[j] = []
+            for a in range(2):
+                first = ((j % 2) * 2 + a) * P
+                c_ps = psum.tile([P, PACK, P], F32, tag="c_ps")
+                for t in range(PACK):
+                    nc.tensor.matmul_mx(
+                        out=c_ps[:, t, :],
+                        lhsT=wc_codes[:, t].rearrange("p g i -> p (g i)").bitcast(FP8X4),
+                        lhsT_scale=wc_planes[:, t].rearrange("p g i -> p (g i)"),
+                        rhs=x_codes[:, first : first + P].bitcast(FP8X4),
+                        rhs_scale=x_scales[:, first : first + P],
+                        start=True,
+                        stop=True,
+                    )
+                c_banks[j].append(c_ps)
+
+        def add_bias(j):
+            grouped = stage.tile([P, 2, P, PACK], BF16, align_bytes=64, name="c_grouped")
+            for a in range(2):
+                nc.vector.tensor_tensor(
+                    out=grouped[:, a],
+                    in0=c_banks[j][a][:].rearrange("p t r -> p r t"),
+                    in1=bias[:].unsqueeze(1).to_broadcast([P, P, PACK]),
+                    op=ADD,
+                )
+            c_grouped[j] = grouped
+
+        def quantise_c(j):
+            c_q[j] = quantise(c_grouped[j], 2, "c")
+
+        def contract(j):
+            c_codes, c_scales = c_q[j]
+            res = res_pool.tile([P, 2, IJ], F32)
+            for h in range(HALVES):
+                o_cols = slice(h * N_OUT, (h + 1) * N_OUT)
+                for a in range(2):
+                    o_ps = psum.tile([P, N_OUT], F32, tag="o_ps", bufs=4)
+                    nc.tensor.matmul_mx(
+                        out=o_ps[:],
+                        lhsT=c_codes[:, a * P : (a + 1) * P].bitcast(FP8X4),
+                        lhsT_scale=c_scales[:, a * P : (a + 1) * P],
+                        rhs=wk_codes[:, o_cols].bitcast(FP8X4),
+                        rhs_scale=wk_scales[:, o_cols],
+                        start=True,
+                        stop=True,
+                    )
+                    if h == 0 and a == 1:
+                        nc.vector.tensor_copy(out=res[:, a, o_cols], in_=o_ps[:])
+                    else:
+                        nc.scalar.copy(out=res[:, a, o_cols], in_=o_ps[:])
+            nc.sync.dma_start(out=out_rows[:, 2 * j : 2 * j + 2, :], in_=res[:])
+
+        transpose_x(0)
 
         wc_codes = keep.tile([P, PACK, HEADS, SUB], I32, align_bytes=64)
         nc.vector.tensor_copy(out=wc_codes[:], in_=wc_raw[:].rearrange("p g (t i) -> p t g i", t=PACK))
@@ -91,89 +184,25 @@ def tile_trittentioncube_pa_t_e_kernel(tc, x, wc_words, wc_scales, b_c, w_k, out
         bias = keep.tile([P, PACK], F32)
         nc.vector.tensor_copy(out=bias[:], in_=bias_t[:, 0:PACK])
 
-        x_q = {}
-        c_q = {}
-
-        def transpose_x(g):
-            x_grouped = stage.tile([P, GROUP, P, PACK], BF16, align_bytes=64)
-            grouped_words = x_grouped[:].bitcast(F32)
-            for half in range(GROUP // 2):
-                x_t = psum.tile([P, 2, 2, P], F32, tag="x_t")
-                for a in range(2):
-                    words = x_sb[g][:, 2 * half + a, :].bitcast(F32)
-                    for u in range(2):
-                        nc.tensor.transpose(x_t[:, a, u, :], words[:, u : D // 2 : 2], ident[:])
-                nc.vector.tensor_copy(
-                    out=grouped_words[:, 2 * half : 2 * half + 2, :, :],
-                    in_=x_t[:].rearrange("p a u r -> p a r u"),
-                )
-            return x_grouped
-
-        def quantise(grouped, held, g, label):
-            q_codes = codes.tile([P, GROUP * P], U32, align_bytes=64, tag=label + "_codes", name=label + "_codes")
-            q_scales = codes.tile([P, GROUP * P], U8, align_bytes=64, tag=label + "_scales", name=label + "_scales")
-            nc.vector.quantize_mx(
-                out=q_codes[:].bitcast(FP8X4),
-                scales=q_scales[:],
-                in_=grouped[:].rearrange("p a r t -> p (a r t)"),
-            )
-            held[g] = (q_codes, q_scales)
-
-        def project(g):
-            x_codes, x_scales = x_q[g]
-            c_grouped = stage.tile([P, GROUP, P, PACK], BF16, align_bytes=64)
-            for a in range(GROUP):
-                cols = slice(a * P, (a + 1) * P)
-                c_ps = psum.tile([P, PACK, P], F32, tag="c_ps")
-                for t in range(PACK):
-                    nc.tensor.matmul_mx(
-                        out=c_ps[:, t, :],
-                        lhsT=wc_codes[:, t].rearrange("p g i -> p (g i)").bitcast(FP8X4),
-                        lhsT_scale=wc_planes[:, t].rearrange("p g i -> p (g i)"),
-                        rhs=x_codes[:, cols].bitcast(FP8X4),
-                        rhs_scale=x_scales[:, cols],
-                        start=True,
-                        stop=True,
-                    )
-                nc.vector.tensor_tensor(
-                    out=c_grouped[:, a],
-                    in0=c_ps[:].rearrange("p t r -> p r t"),
-                    in1=bias[:].unsqueeze(1).to_broadcast([P, P, PACK]),
-                    op=ADD,
-                )
-            return c_grouped
-
-        def contract(g):
-            c_codes, c_scales = c_q[g]
-            for pair in range(GROUP // 2):
-                res = res_pool.tile([P, 2, IJ], F32)
-                for a in range(2):
-                    cols = slice((2 * pair + a) * P, (2 * pair + a + 1) * P)
-                    for h in range(IJ // N_OUT):
-                        o_cols = slice(h * N_OUT, (h + 1) * N_OUT)
-                        o_ps = psum.tile([P, N_OUT], F32, tag="o_ps", bufs=4)
-                        nc.tensor.matmul_mx(
-                            out=o_ps[:],
-                            lhsT=c_codes[:, cols].bitcast(FP8X4),
-                            lhsT_scale=c_scales[:, cols],
-                            rhs=wk_codes[:, o_cols].bitcast(FP8X4),
-                            rhs_scale=wk_scales[:, o_cols],
-                            start=True,
-                            stop=True,
-                        )
-                        nc.scalar.copy(out=res[:, a, o_cols], in_=o_ps[:])
-                first = g * GROUP + 2 * pair
-                nc.sync.dma_start(out=out_rows[:, first : first + 2, :], in_=res[:])
-
-        x_grouped_0 = transpose_x(0)
-        quantise(x_grouped_0, x_q, 0, "x")
+        quantise_x(0)
+        project(0)
+        add_bias(0)
+        quantise_c(0)
+        project(1)
 
         wk_sorted = keep.tile([P, IJ_PER_ROW, 2, HEADS, SUB, 2], BF16)
         for c in range(IJ_PER_ROW):
-            nc.vector.tensor_copy(
-                out=wk_sorted[:, c],
-                in_=wk_raw[:, :, c, :].rearrange("p n (u e i) -> p u n i e", u=2, e=2),
-            )
+            if c % 3 == 1:
+                for u in range(2):
+                    nc.scalar.copy(
+                        out=wk_sorted[:, c, u],
+                        in_=wk_raw[:, :, c, 16 * u : 16 * u + 16].rearrange("p n (e i) -> p n i e", e=2),
+                    )
+            else:
+                nc.vector.tensor_copy(
+                    out=wk_sorted[:, c],
+                    in_=wk_raw[:, :, c, :].rearrange("p n (u e i) -> p u n i e", u=2, e=2),
+                )
         wk_grouped = keep.tile([P, P, IJ_PER_ROW, PACK], BF16, align_bytes=64)
         wk_grouped_words = wk_grouped[:].bitcast(F32)
         for b in range(IJ_PER_ROW // 2):
@@ -189,23 +218,29 @@ def tile_trittentioncube_pa_t_e_kernel(tc, x, wc_words, wc_scales, b_c, w_k, out
                 out=wk_grouped_words[:, :, 2 * b : 2 * b + 2, :],
                 in_=wk_t[:].rearrange("p c u r -> p r c u"),
             )
+        add_bias(1)
+        quantise_c(1)
+        transpose_x(1)
         wk_codes = keep.tile([P, IJ], U32, align_bytes=64)
         wk_scales = keep.tile([P, IJ], U8, align_bytes=64)
-        nc.vector.quantize_mx(
-            out=wk_codes[:].bitcast(FP8X4),
-            scales=wk_scales[:],
-            in_=wk_grouped[:].rearrange("p r c t -> p (r c t)"),
-        )
+        rows = P // HALVES
+        for h in range(HALVES):
+            nc.vector.quantize_mx(
+                out=wk_codes[:, h * N_OUT : (h + 1) * N_OUT].bitcast(FP8X4),
+                scales=wk_scales[:, h * N_OUT : (h + 1) * N_OUT],
+                in_=wk_grouped[:, h * rows : (h + 1) * rows].rearrange("p r c t -> p (r c t)"),
+            )
+        quantise_x(1)
 
-        x_grouped_1 = transpose_x(1)
-        c_grouped_0 = project(0)
-        quantise(x_grouped_1, x_q, 1, "x")
-        quantise(c_grouped_0, c_q, 0, "c")
-        for g in range(GROUPS):
-            x_next = transpose_x(g + 2) if g + 2 < GROUPS else None
-            c_next = project(g + 1) if g + 1 < GROUPS else None
-            if x_next is not None:
-                quantise(x_next, x_q, g + 2, "x")
-            if c_next is not None:
-                quantise(c_next, c_q, g + 1, "c")
-            contract(g)
+        for j in range(PAIRS):
+            if 1 <= j and j + 1 < PAIRS:
+                quantise_c(j + 1)
+            contract(j)
+            ahead = j // 2 + 2
+            if j % 2 == 1 and ahead < GROUPS:
+                quantise_x(ahead)
+            if j + 2 < PAIRS:
+                project(j + 2)
+                add_bias(j + 2)
+            if j % 2 == 0 and ahead < GROUPS:
+                transpose_x(ahead)

@@ -148,10 +148,11 @@ def tile_trittentioncube_pa_t_e_kernel(tc, x, wc_words, wc_scales, b_c, w_k, out
 
         def contract(j):
             c_codes, c_scales = c_q[j]
+            last = j == PAIRS - 1
             res = res_pool.tile([P, 2, IJ], F32)
-            for h in range(HALVES):
-                o_cols = slice(h * N_OUT, (h + 1) * N_OUT)
-                for a in range(2):
+            for a in range(2):
+                for h in range(HALVES):
+                    o_cols = slice(h * N_OUT, (h + 1) * N_OUT)
                     o_ps = psum.tile([P, N_OUT], F32, tag="o_ps", bufs=4)
                     nc.tensor.matmul_mx(
                         out=o_ps[:],
@@ -162,11 +163,14 @@ def tile_trittentioncube_pa_t_e_kernel(tc, x, wc_words, wc_scales, b_c, w_k, out
                         start=True,
                         stop=True,
                     )
-                    if h == 0 and a == 1:
+                    if h == 0 and (a == 0 or last):
                         nc.vector.tensor_copy(out=res[:, a, o_cols], in_=o_ps[:])
                     else:
                         nc.scalar.copy(out=res[:, a, o_cols], in_=o_ps[:])
-            nc.sync.dma_start(out=out_rows[:, 2 * j : 2 * j + 2, :], in_=res[:])
+                if last:
+                    nc.sync.dma_start(out=out_rows[:, 2 * j + a, :], in_=res[:, a, :])
+            if not last:
+                nc.sync.dma_start(out=out_rows[:, 2 * j : 2 * j + 2, :], in_=res[:])
 
         transpose_x(0)
 
@@ -187,7 +191,6 @@ def tile_trittentioncube_pa_t_e_kernel(tc, x, wc_words, wc_scales, b_c, w_k, out
         quantise_x(0)
         project(0)
         add_bias(0)
-        quantise_c(0)
         project(1)
 
         wk_sorted = keep.tile([P, IJ_PER_ROW, 2, HEADS, SUB, 2], BF16)
@@ -203,6 +206,7 @@ def tile_trittentioncube_pa_t_e_kernel(tc, x, wc_words, wc_scales, b_c, w_k, out
                     out=wk_sorted[:, c],
                     in_=wk_raw[:, :, c, :].rearrange("p n (u e i) -> p u n i e", u=2, e=2),
                 )
+        quantise_c(0)
         wk_grouped = keep.tile([P, P, IJ_PER_ROW, PACK], BF16, align_bytes=64)
         wk_grouped_words = wk_grouped[:].bitcast(F32)
         for b in range(IJ_PER_ROW // 2):
@@ -219,7 +223,6 @@ def tile_trittentioncube_pa_t_e_kernel(tc, x, wc_words, wc_scales, b_c, w_k, out
                 in_=wk_t[:].rearrange("p c u r -> p r c u"),
             )
         add_bias(1)
-        quantise_c(1)
         transpose_x(1)
         wk_codes = keep.tile([P, IJ], U32, align_bytes=64)
         wk_scales = keep.tile([P, IJ], U8, align_bytes=64)
@@ -230,12 +233,14 @@ def tile_trittentioncube_pa_t_e_kernel(tc, x, wc_words, wc_scales, b_c, w_k, out
                 scales=wk_scales[:, h * N_OUT : (h + 1) * N_OUT],
                 in_=wk_grouped[:, h * rows : (h + 1) * rows].rearrange("p r c t -> p (r c t)"),
             )
+            if h == 0:
+                quantise_c(1)
         quantise_x(1)
 
         for j in range(PAIRS):
+            contract(j)
             if 1 <= j and j + 1 < PAIRS:
                 quantise_c(j + 1)
-            contract(j)
             ahead = j // 2 + 2
             if j % 2 == 1 and ahead < GROUPS:
                 quantise_x(ahead)

@@ -60,6 +60,11 @@ def tile_trittentioncube_pa_t_e_kernel(tc, x, wc_words, wc_scales, b_c, w_k, out
         make_identity(nc, ident[:])
 
         load_x(0)
+        wk_raw = keep.tile([P, HEADS, IJ_PER_ROW, DH], BF16)
+        nc.sync.dma_start(
+            out=wk_raw[:].rearrange("p n c k -> p n (c k)"),
+            in_=w_k.rearrange("n i j k -> n (i j) k").rearrange("n (r c) k -> r n (c k)", c=IJ_PER_ROW),
+        )
         wc_raw = keep.tile([P, HEADS, DH], I32)
         nc.sync.dma_start(
             out=wc_raw[:],
@@ -72,11 +77,6 @@ def tile_trittentioncube_pa_t_e_kernel(tc, x, wc_words, wc_scales, b_c, w_k, out
                 in_=scale_words[:, 4 * quad : 4 * quad + 4, :].rearrange("g r w -> r g w"),
             )
         nc.sync.dma_start(out=bias_rows[0:PACK], in_=b_c.rearrange("n (t i) -> t n i", i=SUB))
-        wk_raw = keep.tile([P, HEADS, IJ_PER_ROW, DH], BF16)
-        nc.sync.dma_start(
-            out=wk_raw[:].rearrange("p n c k -> p n (c k)"),
-            in_=w_k.rearrange("n i j k -> n (i j) k").rearrange("n (r c) k -> r n (c k)", c=IJ_PER_ROW),
-        )
         for g in range(1, GROUPS):
             load_x(g)
 
@@ -148,6 +148,7 @@ def tile_trittentioncube_pa_t_e_kernel(tc, x, wc_words, wc_scales, b_c, w_k, out
 
         def contract(j):
             c_codes, c_scales = c_q[j]
+            first = j == 0
             last = j == PAIRS - 1
             res = res_pool.tile([P, 2, IJ], F32)
             for a in range(2):
@@ -163,35 +164,17 @@ def tile_trittentioncube_pa_t_e_kernel(tc, x, wc_words, wc_scales, b_c, w_k, out
                         start=True,
                         stop=True,
                     )
-                    if h == 0 and (a == 0 or last):
+                    if h == 0 and ((a == 0 and not first) or last):
                         nc.vector.tensor_copy(out=res[:, a, o_cols], in_=o_ps[:])
                     else:
                         nc.scalar.copy(out=res[:, a, o_cols], in_=o_ps[:])
-                if last:
+                if first or last:
                     nc.sync.dma_start(out=out_rows[:, 2 * j + a, :], in_=res[:, a, :])
-            if not last:
+            if not (first or last):
                 nc.sync.dma_start(out=out_rows[:, 2 * j : 2 * j + 2, :], in_=res[:])
 
         transpose_x(0)
-
-        wc_codes = keep.tile([P, PACK, HEADS, SUB], I32, align_bytes=64)
-        nc.vector.tensor_copy(out=wc_codes[:], in_=wc_raw[:].rearrange("p g (t i) -> p t g i", t=PACK))
-        wc_planes = keep.tile([P, PACK, HEADS, SUB], U8, align_bytes=64)
-        nc.vector.tensor_copy(
-            out=wc_planes[:].bitcast(I32),
-            in_=wcs_raw[:].bitcast(I32).rearrange("p g (t w) -> p t g w", t=PACK),
-        )
-        bias_rows_f32 = keep.tile([P, P], F32)
-        nc.vector.tensor_copy(out=bias_rows_f32[:], in_=bias_rows[:].rearrange("p n i -> p (n i)"))
-        bias_t = psum.tile([P, P], F32, tag="c_ps")
-        nc.tensor.transpose(bias_t[:], bias_rows_f32[:], ident[:])
-        bias = keep.tile([P, PACK], F32)
-        nc.vector.tensor_copy(out=bias[:], in_=bias_t[:, 0:PACK])
-
         quantise_x(0)
-        project(0)
-        add_bias(0)
-        project(1)
 
         wk_sorted = keep.tile([P, IJ_PER_ROW, 2, HEADS, SUB, 2], BF16)
         for c in range(IJ_PER_ROW):
@@ -206,7 +189,6 @@ def tile_trittentioncube_pa_t_e_kernel(tc, x, wc_words, wc_scales, b_c, w_k, out
                     out=wk_sorted[:, c],
                     in_=wk_raw[:, :, c, :].rearrange("p n (u e i) -> p u n i e", u=2, e=2),
                 )
-        quantise_c(0)
         wk_grouped = keep.tile([P, P, IJ_PER_ROW, PACK], BF16, align_bytes=64)
         wk_grouped_words = wk_grouped[:].bitcast(F32)
         for b in range(IJ_PER_ROW // 2):
@@ -222,20 +204,43 @@ def tile_trittentioncube_pa_t_e_kernel(tc, x, wc_words, wc_scales, b_c, w_k, out
                 out=wk_grouped_words[:, :, 2 * b : 2 * b + 2, :],
                 in_=wk_t[:].rearrange("p c u r -> p r c u"),
             )
-        add_bias(1)
+
+        wc_codes = keep.tile([P, PACK, HEADS, SUB], I32, align_bytes=64)
+        nc.vector.tensor_copy(out=wc_codes[:], in_=wc_raw[:].rearrange("p g (t i) -> p t g i", t=PACK))
+        wc_planes = keep.tile([P, PACK, HEADS, SUB], U8, align_bytes=64)
+        nc.vector.tensor_copy(
+            out=wc_planes[:].bitcast(I32),
+            in_=wcs_raw[:].bitcast(I32).rearrange("p g (t w) -> p t g w", t=PACK),
+        )
+        bias_rows_f32 = keep.tile([P, P], F32)
+        nc.vector.tensor_copy(out=bias_rows_f32[:], in_=bias_rows[:].rearrange("p n i -> p (n i)"))
+        bias_t = psum.tile([P, P], F32, tag="c_ps")
+        nc.tensor.transpose(bias_t[:], bias_rows_f32[:], ident[:])
+        bias = keep.tile([P, PACK], F32)
+        nc.vector.tensor_copy(out=bias[:], in_=bias_t[:, 0:PACK])
+
+        project(0)
+        add_bias(0)
         transpose_x(1)
+
         wk_codes = keep.tile([P, IJ], U32, align_bytes=64)
         wk_scales = keep.tile([P, IJ], U8, align_bytes=64)
         rows = P // HALVES
-        for h in range(HALVES):
+
+        def quantise_wk(h):
             nc.vector.quantize_mx(
                 out=wk_codes[:, h * N_OUT : (h + 1) * N_OUT].bitcast(FP8X4),
                 scales=wk_scales[:, h * N_OUT : (h + 1) * N_OUT],
                 in_=wk_grouped[:, h * rows : (h + 1) * rows].rearrange("p r c t -> p (r c t)"),
             )
-            if h == 0:
-                quantise_c(1)
+
+        quantise_wk(0)
+        quantise_c(0)
+        project(1)
+        quantise_wk(1)
+        add_bias(1)
         quantise_x(1)
+        quantise_c(1)
 
         for j in range(PAIRS):
             contract(j)

@@ -54,8 +54,6 @@ def tile_trittentioncube_pa_t_e_kernel(tc, x, wc_words, wc_scales, b_c, w_k, out
 
         wcs_raw = keep.tile([P, HEADS, DH], U8, align_bytes=64)
         nc.vector.memset(wcs_raw[:].rearrange("p g n -> p (g n)").bitcast(I32), 0)
-        bias_rows = keep.tile([P, HEADS, SUB], BF16)
-        nc.vector.memset(bias_rows[:], 0.0)
         ident = keep.tile([P, P], F32)
         make_identity(nc, ident[:])
 
@@ -76,7 +74,8 @@ def tile_trittentioncube_pa_t_e_kernel(tc, x, wc_words, wc_scales, b_c, w_k, out
                 out=wcs_raw[32 * quad : 32 * quad + 4].bitcast(I32),
                 in_=scale_words[:, 4 * quad : 4 * quad + 4, :].rearrange("g r w -> r g w"),
             )
-        nc.sync.dma_start(out=bias_rows[0:PACK], in_=b_c.rearrange("n (t i) -> t n i", i=SUB))
+        bias_bf = keep.tile([P, PACK], BF16)
+        nc.sync.dma_start(out=bias_bf[:], in_=b_c.rearrange("n (i t) -> (n i) t", t=PACK))
         for g in range(1, GROUPS):
             load_x(g)
 
@@ -176,19 +175,12 @@ def tile_trittentioncube_pa_t_e_kernel(tc, x, wc_words, wc_scales, b_c, w_k, out
         transpose_x(0)
         quantise_x(0)
 
-        wk_sorted = keep.tile([P, IJ_PER_ROW, 2, HEADS, SUB, 2], BF16)
-        for c in range(IJ_PER_ROW):
-            if c % 3 == 1:
-                for u in range(2):
-                    nc.scalar.copy(
-                        out=wk_sorted[:, c, u],
-                        in_=wk_raw[:, :, c, 16 * u : 16 * u + 16].rearrange("p n (e i) -> p n i e", e=2),
-                    )
-            else:
-                nc.vector.tensor_copy(
-                    out=wk_sorted[:, c],
-                    in_=wk_raw[:, :, c, :].rearrange("p n (u e i) -> p u n i e", u=2, e=2),
-                )
+        wk_sorted = keep.tile([P, IJ_PER_ROW, HEADS, DH], BF16)
+        for b in range(IJ_PER_ROW // 2):
+            nc.vector.tensor_copy(
+                out=wk_sorted[:, 2 * b : 2 * b + 2],
+                in_=wk_raw[:, :, 2 * b : 2 * b + 2, :].rearrange("p n c k -> p c n k"),
+            )
         wk_grouped = keep.tile([P, P, IJ_PER_ROW, PACK], BF16, align_bytes=64)
         wk_grouped_words = wk_grouped[:].bitcast(F32)
         for b in range(IJ_PER_ROW // 2):
@@ -197,7 +189,7 @@ def tile_trittentioncube_pa_t_e_kernel(tc, x, wc_words, wc_scales, b_c, w_k, out
                 for u in range(2):
                     nc.tensor.transpose(
                         wk_t[:, c2, u, :],
-                        wk_sorted[:, 2 * b + c2, u].rearrange("p n i e -> p (n i e)").bitcast(F32),
+                        wk_sorted[:, 2 * b + c2].rearrange("p n k -> p (n k)").bitcast(F32)[:, u : KC // 2 : 2],
                         ident[:],
                     )
             nc.scalar.copy(
@@ -206,18 +198,14 @@ def tile_trittentioncube_pa_t_e_kernel(tc, x, wc_words, wc_scales, b_c, w_k, out
             )
 
         wc_codes = keep.tile([P, PACK, HEADS, SUB], I32, align_bytes=64)
-        nc.vector.tensor_copy(out=wc_codes[:], in_=wc_raw[:].rearrange("p g (t i) -> p t g i", t=PACK))
+        nc.vector.tensor_copy(out=wc_codes[:], in_=wc_raw[:].rearrange("p g (i t) -> p t g i", t=PACK))
         wc_planes = keep.tile([P, PACK, HEADS, SUB], U8, align_bytes=64)
-        nc.vector.tensor_copy(
-            out=wc_planes[:].bitcast(I32),
-            in_=wcs_raw[:].bitcast(I32).rearrange("p g (t w) -> p t g w", t=PACK),
+        nc.gpsimd.tensor_copy(
+            out=wc_planes[:].rearrange("p t g i -> p g i t"),
+            in_=wcs_raw[:].rearrange("p g (i t) -> p g i t", t=PACK),
         )
-        bias_rows_f32 = keep.tile([P, P], F32)
-        nc.vector.tensor_copy(out=bias_rows_f32[:], in_=bias_rows[:].rearrange("p n i -> p (n i)"))
-        bias_t = psum.tile([P, P], F32, tag="c_ps")
-        nc.tensor.transpose(bias_t[:], bias_rows_f32[:], ident[:])
         bias = keep.tile([P, PACK], F32)
-        nc.vector.tensor_copy(out=bias[:], in_=bias_t[:, 0:PACK])
+        nc.vector.tensor_copy(out=bias[:], in_=bias_bf[:])
 
         project(0)
         add_bias(0)

@@ -56,8 +56,25 @@ def tile_trittentioncube_pa_t_e_kernel(tc, x, wc_words, wc_scales, b_c, w_k, out
         nc.vector.memset(wcs_raw[:].rearrange("p g n -> p (g n)").bitcast(I32), 0)
         ident = keep.tile([P, P], F32)
         make_identity(nc, ident[:])
+        warm_w = keep.tile([P, P], BF16)
+        nc.vector.memset(warm_w[:], 0.0)
+        warm_x = keep.tile([P, N_OUT], BF16)
+        nc.vector.memset(warm_x[:], 0.0)
+
+        def keep_warm(count):
+            unread = psum.tile([P, N_OUT], F32, tag="c_ps")
+            for repeat in range(count):
+                nc.tensor.matmul(out=unread[:], lhsT=warm_w[:], rhs=warm_x[:], start=True, stop=True)
 
         load_x(0)
+        scale_words = wc_scales.bitcast(I32)
+        for quad in range(4):
+            nc.sync.dma_start(
+                out=wcs_raw[32 * quad : 32 * quad + 4].bitcast(I32),
+                in_=scale_words[:, 4 * quad : 4 * quad + 4, :].rearrange("g r w -> r g w"),
+            )
+        bias_bf = keep.tile([P, PACK], BF16)
+        nc.sync.dma_start(out=bias_bf[:], in_=b_c.rearrange("n (i t) -> (n i) t", t=PACK))
         wk_raw = keep.tile([P, HEADS, IJ_PER_ROW, DH], BF16)
         nc.sync.dma_start(
             out=wk_raw[:].rearrange("p n c k -> p n (c k)"),
@@ -68,14 +85,6 @@ def tile_trittentioncube_pa_t_e_kernel(tc, x, wc_words, wc_scales, b_c, w_k, out
             out=wc_raw[:],
             in_=wc_words.rearrange("g p n t -> g p (n t)").bitcast(I32).rearrange("g p n -> p g n"),
         )
-        scale_words = wc_scales.bitcast(I32)
-        for quad in range(4):
-            nc.sync.dma_start(
-                out=wcs_raw[32 * quad : 32 * quad + 4].bitcast(I32),
-                in_=scale_words[:, 4 * quad : 4 * quad + 4, :].rearrange("g r w -> r g w"),
-            )
-        bias_bf = keep.tile([P, PACK], BF16)
-        nc.sync.dma_start(out=bias_bf[:], in_=b_c.rearrange("n (i t) -> (n i) t", t=PACK))
         for g in range(1, GROUPS):
             load_x(g)
 
@@ -172,7 +181,9 @@ def tile_trittentioncube_pa_t_e_kernel(tc, x, wc_words, wc_scales, b_c, w_k, out
             if not (first or last):
                 nc.sync.dma_start(out=out_rows[:, 2 * j : 2 * j + 2, :], in_=res[:])
 
+        keep_warm(6)
         transpose_x(0)
+        keep_warm(6)
         quantise_x(0)
 
         wk_sorted = keep.tile([P, IJ_PER_ROW, HEADS, DH], BF16)
@@ -196,6 +207,8 @@ def tile_trittentioncube_pa_t_e_kernel(tc, x, wc_words, wc_scales, b_c, w_k, out
                 out=wk_grouped_words[:, :, 2 * b : 2 * b + 2, :],
                 in_=wk_t[:].rearrange("p c u r -> p r c u"),
             )
+            if b < IJ_PER_ROW // 2 - 1:
+                keep_warm(2)
 
         wc_codes = keep.tile([P, PACK, HEADS, SUB], I32, align_bytes=64)
         nc.vector.tensor_copy(out=wc_codes[:], in_=wc_raw[:].rearrange("p g (i t) -> p t g i", t=PACK))

@@ -39,7 +39,7 @@ def tile_trittentioncube_pa_t_e_kernel(tc, x, wc_words, wc_scales, b_c, w_k, out
         stage = ctx.enter_context(tc.tile_pool(name="stage", bufs=3))
         codes = ctx.enter_context(tc.tile_pool(name="codes", bufs=4))
         res_pool = ctx.enter_context(tc.tile_pool(name="res", bufs=4))
-        psum = ctx.enter_context(tc.psum_pool(name="psum", bufs=2))
+        psum = ctx.enter_context(tc.psum_pool(name="psum", bufs=8))
         ctx.enter_context(tc.manual_schedule())
 
         x_rows = x.rearrange("b r d -> (b r) d").rearrange("(p s) d -> p s d", s=TILES)
@@ -56,15 +56,6 @@ def tile_trittentioncube_pa_t_e_kernel(tc, x, wc_words, wc_scales, b_c, w_k, out
         nc.vector.memset(wcs_raw[:].rearrange("p g n -> p (g n)").bitcast(I32), 0)
         ident = keep.tile([P, P], F32)
         make_identity(nc, ident[:])
-        warm_w = keep.tile([P, P], BF16)
-        nc.vector.memset(warm_w[:], 0.0)
-        warm_x = keep.tile([P, N_OUT], BF16)
-        nc.vector.memset(warm_x[:], 0.0)
-
-        def keep_warm(count):
-            unread = psum.tile([P, N_OUT], F32, tag="c_ps")
-            for repeat in range(count):
-                nc.tensor.matmul(out=unread[:], lhsT=warm_w[:], rhs=warm_x[:], start=True, stop=True)
 
         load_x(0)
         scale_words = wc_scales.bitcast(I32)
@@ -88,24 +79,32 @@ def tile_trittentioncube_pa_t_e_kernel(tc, x, wc_words, wc_scales, b_c, w_k, out
         for g in range(1, GROUPS):
             load_x(g)
 
+        x_banks = {}
         x_grouped = {}
+        o_banks = {}
+        results = {}
         x_q = {}
         c_banks = {}
         c_grouped = {}
         c_q = {}
 
         def transpose_x(g):
-            grouped = stage.tile([P, GROUP, P, PACK], BF16, align_bytes=64, name="x_grouped")
-            grouped_words = grouped[:].bitcast(F32)
+            x_banks[g] = []
             for half in range(GROUP // 2):
-                x_t = psum.tile([P, 2, 2, P], F32, tag="x_t")
+                x_t = psum.tile([P, 2, 2, P], F32, tag="bank")
                 for a in range(2):
                     words = x_sb[g][:, 2 * half + a, :].bitcast(F32)
                     for u in range(2):
                         nc.tensor.transpose(x_t[:, a, u, :], words[:, u : D // 2 : 2], ident[:])
+                x_banks[g].append(x_t)
+
+        def empty_x(g):
+            grouped = stage.tile([P, GROUP, P, PACK], BF16, align_bytes=64, name="x_grouped")
+            grouped_words = grouped[:].bitcast(F32)
+            for half in range(GROUP // 2):
                 nc.scalar.copy(
                     out=grouped_words[:, 2 * half : 2 * half + 2, :, :],
-                    in_=x_t[:].rearrange("p a u r -> p a r u"),
+                    in_=x_banks[g][half][:].rearrange("p a u r -> p a r u"),
                 )
             x_grouped[g] = grouped
 
@@ -127,7 +126,7 @@ def tile_trittentioncube_pa_t_e_kernel(tc, x, wc_words, wc_scales, b_c, w_k, out
             c_banks[j] = []
             for a in range(2):
                 first = ((j % 2) * 2 + a) * P
-                c_ps = psum.tile([P, PACK, P], F32, tag="c_ps")
+                c_ps = psum.tile([P, PACK, P], F32, tag="bank")
                 for t in range(PACK):
                     nc.tensor.matmul_mx(
                         out=c_ps[:, t, :],
@@ -154,36 +153,32 @@ def tile_trittentioncube_pa_t_e_kernel(tc, x, wc_words, wc_scales, b_c, w_k, out
         def quantise_c(j):
             c_q[j] = quantise(c_grouped[j], 2, "c")
 
-        def contract(j):
+        def contract(j, bank):
             c_codes, c_scales = c_q[j]
-            first = j == 0
-            last = j == PAIRS - 1
-            res = res_pool.tile([P, 2, IJ], F32)
-            for a in range(2):
-                for h in range(HALVES):
-                    o_cols = slice(h * N_OUT, (h + 1) * N_OUT)
-                    o_ps = psum.tile([P, N_OUT], F32, tag="o_ps", bufs=4)
-                    nc.tensor.matmul_mx(
-                        out=o_ps[:],
-                        lhsT=c_codes[:, a * P : (a + 1) * P].bitcast(FP8X4),
-                        lhsT_scale=c_scales[:, a * P : (a + 1) * P],
-                        rhs=wk_codes[:, o_cols].bitcast(FP8X4),
-                        rhs_scale=wk_scales[:, o_cols],
-                        start=True,
-                        stop=True,
-                    )
-                    if h == 0 and ((a == 0 and not first) or last):
-                        nc.vector.tensor_copy(out=res[:, a, o_cols], in_=o_ps[:])
-                    else:
-                        nc.scalar.copy(out=res[:, a, o_cols], in_=o_ps[:])
-                if first or last:
-                    nc.sync.dma_start(out=out_rows[:, 2 * j + a, :], in_=res[:, a, :])
-            if not (first or last):
-                nc.sync.dma_start(out=out_rows[:, 2 * j : 2 * j + 2, :], in_=res[:])
+            a, h = divmod(bank, HALVES)
+            o_ps = psum.tile([P, N_OUT], F32, tag="bank")
+            nc.tensor.matmul_mx(
+                out=o_ps[:],
+                lhsT=c_codes[:, a * P : (a + 1) * P].bitcast(FP8X4),
+                lhsT_scale=c_scales[:, a * P : (a + 1) * P],
+                rhs=wk_codes[:, h * N_OUT : (h + 1) * N_OUT].bitcast(FP8X4),
+                rhs_scale=wk_scales[:, h * N_OUT : (h + 1) * N_OUT],
+                start=True,
+                stop=True,
+            )
+            o_banks[j, bank] = o_ps
 
-        keep_warm(6)
+        def empty(j, bank, copy):
+            if j not in results:
+                results[j] = res_pool.tile([P, 2, IJ], F32, name="res")
+            a, h = divmod(bank, HALVES)
+            copy(out=results[j][:, a, h * N_OUT : (h + 1) * N_OUT], in_=o_banks[j, bank][:])
+
+        def store(j):
+            nc.sync.dma_start(out=out_rows[:, 2 * j : 2 * j + 2, :], in_=results[j][:])
+
         transpose_x(0)
-        keep_warm(6)
+        empty_x(0)
         quantise_x(0)
 
         wk_sorted = keep.tile([P, IJ_PER_ROW, HEADS, DH], BF16)
@@ -195,7 +190,7 @@ def tile_trittentioncube_pa_t_e_kernel(tc, x, wc_words, wc_scales, b_c, w_k, out
         wk_grouped = keep.tile([P, P, IJ_PER_ROW, PACK], BF16, align_bytes=64)
         wk_grouped_words = wk_grouped[:].bitcast(F32)
         for b in range(IJ_PER_ROW // 2):
-            wk_t = psum.tile([P, 2, 2, P], F32, tag="o_ps", bufs=4)
+            wk_t = psum.tile([P, 2, 2, P], F32, tag="bank")
             for c2 in range(2):
                 for u in range(2):
                     nc.tensor.transpose(
@@ -207,8 +202,6 @@ def tile_trittentioncube_pa_t_e_kernel(tc, x, wc_words, wc_scales, b_c, w_k, out
                 out=wk_grouped_words[:, :, 2 * b : 2 * b + 2, :],
                 in_=wk_t[:].rearrange("p c u r -> p r c u"),
             )
-            if b < IJ_PER_ROW // 2 - 1:
-                keep_warm(2)
 
         wc_codes = keep.tile([P, PACK, HEADS, SUB], I32, align_bytes=64)
         nc.vector.tensor_copy(out=wc_codes[:], in_=wc_raw[:].rearrange("p g (i t) -> p t g i", t=PACK))
@@ -223,6 +216,7 @@ def tile_trittentioncube_pa_t_e_kernel(tc, x, wc_words, wc_scales, b_c, w_k, out
         project(0)
         add_bias(0)
         transpose_x(1)
+        empty_x(1)
 
         wk_codes = keep.tile([P, IJ], U32, align_bytes=64)
         wk_scales = keep.tile([P, IJ], U8, align_bytes=64)
@@ -244,14 +238,28 @@ def tile_trittentioncube_pa_t_e_kernel(tc, x, wc_words, wc_scales, b_c, w_k, out
         quantise_c(1)
 
         for j in range(PAIRS):
-            contract(j)
+            ahead = j // 2 + 2
+            new_x = j % 2 == 0 and ahead < GROUPS
+            contract(j, 0)
+            if new_x:
+                transpose_x(ahead)
+            if j + 2 < PAIRS:
+                project(j + 2)
+            for bank in (1, 2, 3):
+                contract(j, bank)
             if 1 <= j and j + 1 < PAIRS:
                 quantise_c(j + 1)
-            ahead = j // 2 + 2
             if j % 2 == 1 and ahead < GROUPS:
                 quantise_x(ahead)
             if j + 2 < PAIRS:
-                project(j + 2)
                 add_bias(j + 2)
-            if j % 2 == 0 and ahead < GROUPS:
-                transpose_x(ahead)
+            empty(j, 2, nc.vector.tensor_copy)
+            if j == PAIRS - 1:
+                empty(j, 0, nc.vector.tensor_copy)
+            if j < PAIRS - 1:
+                empty(j, 0, nc.scalar.copy)
+            if new_x:
+                empty_x(ahead)
+            empty(j, 1, nc.scalar.copy)
+            empty(j, 3, nc.scalar.copy)
+            store(j)

from contextlib import ExitStack

import concourse.mybir as mybir
from concourse.masks import make_identity

F32 = mybir.dt.float32
BF16 = mybir.dt.bfloat16
I32 = mybir.dt.int32
U32 = mybir.dt.uint32
U8 = mybir.dt.uint8
FP8X4 = mybir.dt.float8_e4m3fn_x4
ADD = mybir.AluOpType.add

P = 128
PACK = 4
TOKENS = 4096
D = 512
HEADS = 16
DH = 32
KC = HEADS * DH
IJ = DH * DH
TILES = TOKENS // P
GROUP = 4
GROUPS = TILES // GROUP
PAIRS = TILES // 2
SUB = DH // PACK
N_OUT = 512
HALVES = IJ // N_OUT
IJ_PER_ROW = IJ // P

FLOPS = 2 * TOKENS * D * KC + 2 * TOKENS * KC * IJ


def tile_trittentioncube_pa_t_e_kernel(tc, x, wc_words, wc_scales, b_c, w_k, out):
    nc = tc.nc
    with ExitStack() as ctx:
        keep = ctx.enter_context(tc.tile_pool(name="keep", bufs=1))
        x_pool = ctx.enter_context(tc.tile_pool(name="x", bufs=GROUPS))
        stage = ctx.enter_context(tc.tile_pool(name="stage", bufs=3))
        codes = ctx.enter_context(tc.tile_pool(name="codes", bufs=4))
        res_pool = ctx.enter_context(tc.tile_pool(name="res", bufs=4))
        psum = ctx.enter_context(tc.psum_pool(name="psum", bufs=8))
        ctx.enter_context(tc.manual_schedule())

        x_rows = x.rearrange("b r d -> (b r) d").rearrange("(p s) d -> p s d", s=TILES)
        out_rows = out.rearrange("b r i j -> (b r) (i j)").rearrange("(p s) c -> p s c", s=TILES)

        x_sb = {}

        def load_x(g):
            x_tile = x_pool.tile([P, GROUP, D], BF16)
            nc.sync.dma_start(out=x_tile[:], in_=x_rows[:, g * GROUP : (g + 1) * GROUP, :])
            x_sb[g] = x_tile

        wcs_raw = keep.tile([P, HEADS, DH], U8, align_bytes=64)
        nc.vector.memset(wcs_raw[:].rearrange("p g n -> p (g n)").bitcast(I32), 0)
        ident = keep.tile([P, P], F32)
        make_identity(nc, ident[:])

        load_x(0)
        scale_words = wc_scales.bitcast(I32)
        for quad in range(4):
            nc.sync.dma_start(
                out=wcs_raw[32 * quad : 32 * quad + 4].bitcast(I32),
                in_=scale_words[:, 4 * quad : 4 * quad + 4, :].rearrange("g r w -> r g w"),
            )
        bias_bf = keep.tile([P, PACK], BF16)
        nc.sync.dma_start(out=bias_bf[:], in_=b_c.rearrange("n (i t) -> (n i) t", t=PACK))
        wk_raw = keep.tile([P, HEADS, IJ_PER_ROW, DH], BF16)
        nc.sync.dma_start(
            out=wk_raw[:].rearrange("p n c k -> p n (c k)"),
            in_=w_k.rearrange("n i j k -> n (i j) k").rearrange("n (r c) k -> r n (c k)", c=IJ_PER_ROW),
        )
        wc_raw = keep.tile([P, HEADS, DH], I32)
        nc.sync.dma_start(
            out=wc_raw[:],
            in_=wc_words.rearrange("g p n t -> g p (n t)").bitcast(I32).rearrange("g p n -> p g n"),
        )
        for g in range(1, GROUPS):
            load_x(g)

        x_banks = {}
        x_grouped = {}
        o_banks = {}
        results = {}
        x_q = {}
        c_banks = {}
        c_grouped = {}
        c_q = {}

        def transpose_x(g):
            x_banks[g] = []
            for half in range(GROUP // 2):
                x_t = psum.tile([P, 2, 2, P], F32, tag="bank")
                for a in range(2):
                    words = x_sb[g][:, 2 * half + a, :].bitcast(F32)
                    for u in range(2):
                        nc.tensor.transpose(x_t[:, a, u, :], words[:, u : D // 2 : 2], ident[:])
                x_banks[g].append(x_t)

        def empty_x(g):
            grouped = stage.tile([P, GROUP, P, PACK], BF16, align_bytes=64, name="x_grouped")
            grouped_words = grouped[:].bitcast(F32)
            for half in range(GROUP // 2):
                nc.scalar.copy(
                    out=grouped_words[:, 2 * half : 2 * half + 2, :, :],
                    in_=x_banks[g][half][:].rearrange("p a u r -> p a r u"),
                )
            x_grouped[g] = grouped

        def quantise(grouped, tiles, label):
            q_codes = codes.tile([P, tiles * P], U32, align_bytes=64, name=label + "_codes")
            q_scales = codes.tile([P, tiles * P], U8, align_bytes=64, name=label + "_scales")
            nc.vector.quantize_mx(
                out=q_codes[:].bitcast(FP8X4),
                scales=q_scales[:],
                in_=grouped[:].rearrange("p a r t -> p (a r t)"),
            )
            return q_codes, q_scales

        def quantise_x(g):
            x_q[g] = quantise(x_grouped[g], GROUP, "x")

        def project(j):
            x_codes, x_scales = x_q[j // 2]
            c_banks[j] = []
            for a in range(2):
                first = ((j % 2) * 2 + a) * P
                c_ps = psum.tile([P, PACK, P], F32, tag="bank")
                for t in range(PACK):
                    nc.tensor.matmul_mx(
                        out=c_ps[:, t, :],
                        lhsT=wc_codes[:, t].rearrange("p g i -> p (g i)").bitcast(FP8X4),
                        lhsT_scale=wc_planes[:, t].rearrange("p g i -> p (g i)"),
                        rhs=x_codes[:, first : first + P].bitcast(FP8X4),
                        rhs_scale=x_scales[:, first : first + P],
                        start=True,
                        stop=True,
                    )
                c_banks[j].append(c_ps)

        def add_bias(j):
            grouped = stage.tile([P, 2, P, PACK], BF16, align_bytes=64, name="c_grouped")
            for a in range(2):
                nc.vector.tensor_tensor(
                    out=grouped[:, a],
                    in0=c_banks[j][a][:].rearrange("p t r -> p r t"),
                    in1=bias[:].unsqueeze(1).to_broadcast([P, P, PACK]),
                    op=ADD,
                )
            c_grouped[j] = grouped

        def quantise_c(j):
            c_q[j] = quantise(c_grouped[j], 2, "c")

        def contract(j, bank):
            c_codes, c_scales = c_q[j]
            a, h = divmod(bank, HALVES)
            o_ps = psum.tile([P, N_OUT], F32, tag="bank")
            nc.tensor.matmul_mx(
                out=o_ps[:],
                lhsT=c_codes[:, a * P : (a + 1) * P].bitcast(FP8X4),
                lhsT_scale=c_scales[:, a * P : (a + 1) * P],
                rhs=wk_codes[:, h * N_OUT : (h + 1) * N_OUT].bitcast(FP8X4),
                rhs_scale=wk_scales[:, h * N_OUT : (h + 1) * N_OUT],
                start=True,
                stop=True,
            )
            o_banks[j, bank] = o_ps

        def empty(j, bank, copy):
            if j not in results:
                results[j] = res_pool.tile([P, 2, IJ], F32, name="res")
            a, h = divmod(bank, HALVES)
            copy(out=results[j][:, a, h * N_OUT : (h + 1) * N_OUT], in_=o_banks[j, bank][:])

        def store(j):
            nc.sync.dma_start(out=out_rows[:, 2 * j : 2 * j + 2, :], in_=results[j][:])

        transpose_x(0)
        empty_x(0)
        quantise_x(0)

        wk_sorted = keep.tile([P, IJ_PER_ROW, HEADS, DH], BF16)
        for b in range(IJ_PER_ROW // 2):
            nc.vector.tensor_copy(
                out=wk_sorted[:, 2 * b : 2 * b + 2],
                in_=wk_raw[:, :, 2 * b : 2 * b + 2, :].rearrange("p n c k -> p c n k"),
            )
        wk_grouped = keep.tile([P, P, IJ_PER_ROW, PACK], BF16, align_bytes=64)
        wk_grouped_words = wk_grouped[:].bitcast(F32)
        for b in range(IJ_PER_ROW // 2):
            wk_t = psum.tile([P, 2, 2, P], F32, tag="bank")
            for c2 in range(2):
                for u in range(2):
                    nc.tensor.transpose(
                        wk_t[:, c2, u, :],
                        wk_sorted[:, 2 * b + c2].rearrange("p n k -> p (n k)").bitcast(F32)[:, u : KC // 2 : 2],
                        ident[:],
                    )
            nc.scalar.copy(
                out=wk_grouped_words[:, :, 2 * b : 2 * b + 2, :],
                in_=wk_t[:].rearrange("p c u r -> p r c u"),
            )

        wc_codes = keep.tile([P, PACK, HEADS, SUB], I32, align_bytes=64)
        nc.vector.tensor_copy(out=wc_codes[:], in_=wc_raw[:].rearrange("p g (i t) -> p t g i", t=PACK))
        wc_planes = keep.tile([P, PACK, HEADS, SUB], U8, align_bytes=64)
        nc.gpsimd.tensor_copy(
            out=wc_planes[:].rearrange("p t g i -> p g i t"),
            in_=wcs_raw[:].rearrange("p g (i t) -> p g i t", t=PACK),
        )
        bias = keep.tile([P, PACK], F32)
        nc.vector.tensor_copy(out=bias[:], in_=bias_bf[:])

        project(0)
        add_bias(0)
        transpose_x(1)
        empty_x(1)

        wk_codes = keep.tile([P, IJ], U32, align_bytes=64)
        wk_scales = keep.tile([P, IJ], U8, align_bytes=64)
        rows = P // HALVES

        def quantise_wk(h):
            nc.vector.quantize_mx(
                out=wk_codes[:, h * N_OUT : (h + 1) * N_OUT].bitcast(FP8X4),
                scales=wk_scales[:, h * N_OUT : (h + 1) * N_OUT],
                in_=wk_grouped[:, h * rows : (h + 1) * rows].rearrange("p r c t -> p (r c t)"),
            )

        quantise_wk(0)
        quantise_c(0)
        project(1)
        quantise_wk(1)
        add_bias(1)
        quantise_x(1)
        quantise_c(1)

        for j in range(PAIRS):
            ahead = j // 2 + 2
            new_x = j % 2 == 0 and ahead < GROUPS
            contract(j, 0)
            if new_x:
                transpose_x(ahead)
            if j + 2 < PAIRS:
                project(j + 2)
            for bank in (1, 2, 3):
                contract(j, bank)
            if 1 <= j and j + 1 < PAIRS:
                quantise_c(j + 1)
            if j % 2 == 1 and ahead < GROUPS:
                quantise_x(ahead)
            if j + 2 < PAIRS:
                add_bias(j + 2)
            empty(j, 2, nc.vector.tensor_copy)
            if j == PAIRS - 1:
                empty(j, 0, nc.vector.tensor_copy)
            if j < PAIRS - 1:
                empty(j, 0, nc.scalar.copy)
            if new_x:
                empty_x(ahead)
            empty(j, 1, nc.scalar.copy)
            empty(j, 3, nc.scalar.copy)
            store(j)
